import numpy as np
import ml_dtypes


def mxq(x, axis, fmt="e4m3"):
    dtype, down = {"e4m3": (ml_dtypes.float8_e4m3fn, 7), "e5m2": (ml_dtypes.float8_e5m2, 14)}[fmt]
    v = np.moveaxis(np.asarray(x, np.float32).astype(ml_dtypes.bfloat16).astype(np.float64), axis, -1)
    blocks = v.reshape(v.shape[:-1] + (-1, 32))
    amax = np.abs(blocks).max(-1, keepdims=True)
    byte = np.maximum(np.where(amax > 0, np.frexp(amax)[1] - 1 + 127, 0) - down, 1)
    scale = np.exp2(byte - 127.0)
    codes = (blocks / scale).astype(np.float32).astype(dtype).astype(np.float64)
    return np.moveaxis((codes * scale).reshape(v.shape), -1, axis)


WIDE = False


def mx_kscale(k):
    if not WIDE:
        return np.ones(k)
    levels = np.array([10, -10, 5, -5, 0])
    a = np.random.permutation(np.resize(levels, k // 512 * 4)).reshape(k // 512, 4)
    idx = np.arange(k)
    return np.exp2(a[idx // 512, idx % 128 // 32])


BF16 = ml_dtypes.bfloat16


def bf(x):
    return np.asarray(x, np.float32).astype(BF16)


def f64(x):
    return np.asarray(x).astype(np.float64)


B, T, V, C, H, R, G = 4, 1024, 512, 512, 4, 128, 512
EPS = 1e-12


def l2norm(u):
    n = np.sqrt(np.sum(u * u, axis=-1, keepdims=True))
    return u / np.maximum(n, EPS)


def setup_inputs():
    s = mx_kscale(V)
    return {"x": bf(np.random.standard_normal((B, T, V)) * s),
            "basis": bf(np.random.standard_normal((V, R)) / s[:, None]),
            "shared_q_w": bf(np.random.standard_normal((V, C)) / np.sqrt(V) / s[:, None]),
            "shared_k_w": bf(np.random.standard_normal((V, C)) / np.sqrt(V) / s[:, None]),
            "v_coeffs": bf(np.random.standard_normal((C, R)) * 3.0 / np.sqrt(V * R))}


def reference(x, basis, shared_q_w, shared_k_w, v_coeffs):
    v_w = f64(basis) @ f64(v_coeffs).T
    xq = mxq(f64(x), 2, "e4m3")
    q = l2norm(xq @ mxq(f64(shared_q_w), 0, "e4m3"))
    k = l2norm(xq @ mxq(f64(shared_k_w), 0, "e4m3"))
    v = xq @ mxq(v_w, 0, "e4m3")
    return q, k, v

@@ -1,0 +1,196 @@
+from contextlib import ExitStack
+
+import concourse.mybir as mybir
+from concourse.masks import make_identity
+
+F32 = mybir.dt.float32
+BF16 = mybir.dt.bfloat16
+U32 = mybir.dt.uint32
+U8 = mybir.dt.uint8
+FP8X4 = mybir.dt.float8_e4m3fn_x4
+ALU = mybir.AluOpType
+ACT = mybir.ActivationFunctionType
+
+P = 128
+PACK = 4
+K = P * PACK
+C = 512
+R = 128
+TOKENS = 4 * 1024
+N_TILES = TOKENS // P
+PAIR = 2
+N_PAIRS = N_TILES // PAIR
+X_LOAD_TILES = 4
+EPS = 1e-12
+
+FLOPS = 3 * 2 * TOKENS * K * C + 2 * K * C * R
+
+
+def tile_multiheadassociativememory_pa_kernel(
+    tc, x, basis, shared_q_w, shared_k_w, v_coeffs, out_0, out_1, out_2
+):
+    nc = tc.nc
+
+    x_rows = x.flatten_outer_dims().rearrange("(p n) k -> p n k", n=N_TILES)
+    q_rows = out_0.flatten_outer_dims().rearrange("(p n) c -> p n c", n=N_TILES)
+    k_rows = out_1.flatten_outer_dims().rearrange("(p n) c -> p n c", n=N_TILES)
+    v_rows = out_2.flatten_outer_dims().rearrange("(p n) c -> p n c", n=N_TILES)
+
+    with ExitStack() as ctx:
+        keep = ctx.enter_context(tc.tile_pool(name="keep", bufs=1))
+        xq_pool = ctx.enter_context(tc.tile_pool(name="xq", bufs=3))
+        out_pool = ctx.enter_context(tc.tile_pool(name="outp", bufs=4))
+        norm_pool = ctx.enter_context(tc.tile_pool(name="norm", bufs=4))
+        turn_psum = ctx.enter_context(tc.psum_pool(name="turn", bufs=1))
+        acc_psum = ctx.enter_context(tc.psum_pool(name="acc", bufs=7))
+
+        def load_k_rows(rows, width, name):
+            raw = keep.tile([P, PACK, width], BF16, name=name)
+            nc.sync.dma_start(
+                out=raw[:].rearrange("p (u e) w -> p u e w", u=2),
+                in_=rows.rearrange("(u p e) w -> p u e w", u=2, e=2),
+            )
+            return raw
+
+        basis_sb = load_k_rows(basis, R, "basis_sb")
+        coeff_sb = keep.tile([P, C // P, R], BF16)
+        nc.sync.dma_start(out=coeff_sb[:], in_=v_coeffs.rearrange("(a p) r -> p a r", p=P))
+        q_raw = load_k_rows(shared_q_w, C, "q_raw")
+        x_sb = []
+        for load in range(N_TILES // X_LOAD_TILES):
+            x_part = keep.tile([P, X_LOAD_TILES * K], BF16, name="x_sb%d" % load)
+            nc.sync.dma_start(
+                out=x_part[:].rearrange("p (n k) -> p n k", k=K),
+                in_=x_rows[:, load * X_LOAD_TILES : (load + 1) * X_LOAD_TILES, :],
+            )
+            x_sb.append(x_part)
+            if load == 0:
+                k_raw = load_k_rows(shared_k_w, C, "k_raw")
+
+        ident_bf16 = keep.tile([P, P], BF16)
+        make_identity(nc, ident_bf16[:])
+        ident_f32 = keep.tile([P, P], F32)
+        make_identity(nc, ident_f32[:])
+        minus_half = keep.tile([P, 2], F32)
+        nc.gpsimd.memset(minus_half[:], -0.5)
+
+        def turn_pair(pair):
+            turned = turn_psum.tile([P, PAIR * 2 * P], F32, tag="turn")
+            for i in range(PAIR):
+                n = pair * PAIR + i
+                words = x_sb[n // X_LOAD_TILES][:].bitcast(F32)
+                first = (n % X_LOAD_TILES) * (K // 2)
+                for u in range(2):
+                    nc.tensor.transpose(
+                        turned[:, (2 * i + u) * P : (2 * i + u + 1) * P],
+                        words[:, first + u * P : first + (u + 1) * P],
+                        ident_f32[:],
+                    )
+            grouped = xq_pool.tile([P, PAIR * P * PACK], BF16, align_bytes=64, name="x_grouped")
+            nc.vector.tensor_copy(
+                out=grouped[:].bitcast(F32).rearrange("p (i r u) -> p i r u", i=PAIR, u=2),
+                in_=turned[:].rearrange("p (i u r) -> p i r u", i=PAIR, u=2),
+            )
+            return grouped
+
+        def quantise_pair(grouped):
+            codes = xq_pool.tile([P, PAIR * P], U32, align_bytes=64, name="x_codes")
+            scales = xq_pool.tile([P, PAIR * P], U8, align_bytes=64, name="x_scales")
+            nc.vector.quantize_mx(out=codes[:].bitcast(FP8X4), scales=scales[:], in_=grouped[:])
+            return codes, scales
+
+        def regroup_weight(copy, raw, name):
+            grouped = keep.tile([P, C, PACK], BF16, align_bytes=64, name=name)
+            copy(
+                out=grouped[:].rearrange("p (c i) t -> p c t i", i=4),
+                in_=raw[:].rearrange("p t (c i) -> p c t i", i=4),
+            )
+            return grouped
+
+        def quantise_weight(grouped, name):
+            codes = keep.tile([P, C], U32, align_bytes=64, name=name + "_codes")
+            scales = keep.tile([P, C], U8, align_bytes=64, name=name + "_scales")
+            nc.vector.quantize_mx(
+                out=codes[:].bitcast(FP8X4),
+                scales=scales[:],
+                in_=grouped[:].rearrange("p c t -> p (c t)"),
+            )
+            return codes, scales
+
+        factors_ps = turn_psum.tile([P, 2 * PACK, P], BF16, tag="turn")
+        for t in range(PACK):
+            nc.tensor.transpose(factors_ps[:, t, :], basis_sb[:, t, :], ident_bf16[:])
+        for a in range(C // P):
+            nc.tensor.transpose(factors_ps[:, PACK + a, :], coeff_sb[:, a, :], ident_bf16[:])
+        factors = keep.tile([P, 2 * PACK, P], BF16)
+        nc.scalar.copy(out=factors[:], in_=factors_ps[:])
+
+        q_grouped = regroup_weight(nc.vector.tensor_copy, q_raw, "q_grouped")
+        x_grouped = turn_pair(0)
+        q_mx = quantise_weight(q_grouped, "q")
+        x_mx = quantise_pair(x_grouped)
+
+        v_raw = keep.tile([P, PACK, C], BF16)
+        for t in range(PACK):
+            v_w_ps = acc_psum.tile([P, C], F32, tag="acc")
+            nc.tensor.matmul(
+                v_w_ps[:],
+                lhsT=factors[:, t, :],
+                rhs=factors[:, PACK:, :].rearrange("p a c -> p (a c)"),
+                start=True,
+                stop=True,
+            )
+            nc.scalar.copy(out=v_raw[:, t, :], in_=v_w_ps[:])
+
+        k_grouped = regroup_weight(nc.scalar.copy, k_raw, "k_grouped")
+        v_grouped = regroup_weight(nc.vector.tensor_copy, v_raw, "v_grouped")
+        k_mx = quantise_weight(k_grouped, "k")
+        v_mx = quantise_weight(v_grouped, "v")
+
+        def product(weight_mx, x_codes, x_scales, i):
+            acc = acc_psum.tile([P, C], F32, tag="acc")
+            nc.tensor.matmul_mx(
+                out=acc[:],
+                lhsT=x_codes[:, i * P : (i + 1) * P].bitcast(FP8X4),
+                lhsT_scale=x_scales[:, i * P : (i + 1) * P],
+                rhs=weight_mx[0][:].bitcast(FP8X4),
+                rhs_scale=weight_mx[1][:],
+                start=True,
+                stop=True,
+            )
+            return acc
+
+        for pair in range(N_PAIRS):
+            if pair + 1 < N_PAIRS:
+                next_grouped = turn_pair(pair + 1)
+            q_out = out_pool.tile([P, PAIR, C], F32)
+            k_out = out_pool.tile([P, PAIR, C], F32)
+            v_out = out_pool.tile([P, PAIR, C], F32)
+            for i in range(PAIR):
+                q_ps = product(q_mx, x_mx[0], x_mx[1], i)
+                k_ps = product(k_mx, x_mx[0], x_mx[1], i)
+                v_ps = product(v_mx, x_mx[0], x_mx[1], i)
+
+                sumsq = norm_pool.tile([P, 2], F32)
+                q_sq = norm_pool.tile([P, C], BF16)
+                nc.scalar.activation(out=q_sq[:], in_=q_ps[:], func=ACT.Square, accum_out=sumsq[:, 0:1])
+                k_sq = norm_pool.tile([P, C], BF16)
+                nc.scalar.activation(out=k_sq[:], in_=k_ps[:], func=ACT.Square, accum_out=sumsq[:, 1:2])
+                nc.scalar.copy(out=v_out[:, i, :], in_=v_ps[:])
+
+                floored = norm_pool.tile([P, 2], F32)
+                nc.gpsimd.tensor_scalar_max(out=floored[:], in0=sumsq[:], scalar1=EPS * EPS)
+                inv_norm = norm_pool.tile([P, 2], F32)
+                nc.gpsimd.tensor_tensor(out=inv_norm[:], in0=floored[:], in1=minus_half[:], op=ALU.pow)
+
+                nc.vector.tensor_scalar_mul(out=q_out[:, i, :], in0=q_ps[:], scalar1=inv_norm[:, 0:1])
+                nc.vector.tensor_scalar_mul(out=k_out[:, i, :], in0=k_ps[:], scalar1=inv_norm[:, 1:2])
+                if i == 0 and pair + 1 < N_PAIRS:
+                    next_mx = quantise_pair(next_grouped)
+
+            tiles = slice(pair * PAIR, (pair + 1) * PAIR)
+            nc.sync.dma_start(out=q_rows[:, tiles, :], in_=q_out[:])
+            nc.sync.dma_start(out=k_rows[:, tiles, :], in_=k_out[:])
+            nc.sync.dma_start(out=v_rows[:, tiles, :], in_=v_out[:])
+            if pair + 1 < N_PAIRS:
+                x_mx = next_mx

@@ -42,7 +42,8 @@ def tile_multiheadassociativememory_pa_kernel(
         out_pool = ctx.enter_context(tc.tile_pool(name="outp", bufs=4))
         norm_pool = ctx.enter_context(tc.tile_pool(name="norm", bufs=4))
         turn_psum = ctx.enter_context(tc.psum_pool(name="turn", bufs=1))
-        acc_psum = ctx.enter_context(tc.psum_pool(name="acc", bufs=7))
+        qk_psum = ctx.enter_context(tc.psum_pool(name="qk", bufs=6))
+        v_psum = ctx.enter_context(tc.psum_pool(name="v", bufs=1))
 
         def load_k_rows(rows, width, name):
             raw = keep.tile([P, PACK, width], BF16, name=name)
@@ -132,7 +133,7 @@ def tile_multiheadassociativememory_pa_kernel(
 
         v_raw = keep.tile([P, PACK, C], BF16)
         for t in range(PACK):
-            v_w_ps = acc_psum.tile([P, C], F32, tag="acc")
+            v_w_ps = qk_psum.tile([P, C], F32, tag="qk")
             nc.tensor.matmul(
                 v_w_ps[:],
                 lhsT=factors[:, t, :],
@@ -147,8 +148,8 @@ def tile_multiheadassociativememory_pa_kernel(
         k_mx = quantise_weight(k_grouped, "k")
         v_mx = quantise_weight(v_grouped, "v")
 
-        def product(weight_mx, x_codes, x_scales, i):
-            acc = acc_psum.tile([P, C], F32, tag="acc")
+        def product(psum, tag, weight_mx, x_codes, x_scales, i):
+            acc = psum.tile([P, C], F32, tag=tag)
             nc.tensor.matmul_mx(
                 out=acc[:],
                 lhsT=x_codes[:, i * P : (i + 1) * P].bitcast(FP8X4),
@@ -167,9 +168,9 @@ def tile_multiheadassociativememory_pa_kernel(
             k_out = out_pool.tile([P, PAIR, C], F32)
             v_out = out_pool.tile([P, PAIR, C], F32)
             for i in range(PAIR):
-                q_ps = product(q_mx, x_mx[0], x_mx[1], i)
-                k_ps = product(k_mx, x_mx[0], x_mx[1], i)
-                v_ps = product(v_mx, x_mx[0], x_mx[1], i)
+                q_ps = product(qk_psum, "qk", q_mx, x_mx[0], x_mx[1], i)
+                k_ps = product(qk_psum, "qk", k_mx, x_mx[0], x_mx[1], i)
+                v_ps = product(v_psum, "v", v_mx, x_mx[0], x_mx[1], i)
 
                 sumsq = norm_pool.tile([P, 2], F32)
                 q_sq = norm_pool.tile([P, C], BF16)

@@ -20,6 +20,7 @@ TOKENS = 4 * 1024
 N_TILES = TOKENS // P
 PAIR = 2
 N_PAIRS = N_TILES // PAIR
+AHEAD = 2
 X_LOAD_TILES = 4
 EPS = 1e-12
 
@@ -38,12 +39,12 @@ def tile_multiheadassociativememory_pa_kernel(
 
     with ExitStack() as ctx:
         keep = ctx.enter_context(tc.tile_pool(name="keep", bufs=1))
-        xq_pool = ctx.enter_context(tc.tile_pool(name="xq", bufs=3))
+        xq_pool = ctx.enter_context(tc.tile_pool(name="xq", bufs=AHEAD + 2))
         out_pool = ctx.enter_context(tc.tile_pool(name="outp", bufs=4))
         norm_pool = ctx.enter_context(tc.tile_pool(name="norm", bufs=4))
         turn_psum = ctx.enter_context(tc.psum_pool(name="turn", bufs=1))
-        qk_psum = ctx.enter_context(tc.psum_pool(name="qk", bufs=6))
-        v_psum = ctx.enter_context(tc.psum_pool(name="v", bufs=1))
+        acc_psum = ctx.enter_context(tc.psum_pool(name="acc", bufs=7))
+        ctx.enter_context(tc.manual_schedule())
 
         def load_k_rows(rows, width, name):
             raw = keep.tile([P, PACK, width], BF16, name=name)
@@ -57,6 +58,7 @@ def tile_multiheadassociativememory_pa_kernel(
         coeff_sb = keep.tile([P, C // P, R], BF16)
         nc.sync.dma_start(out=coeff_sb[:], in_=v_coeffs.rearrange("(a p) r -> p a r", p=P))
         q_raw = load_k_rows(shared_q_w, C, "q_raw")
+        k_raw = load_k_rows(shared_k_w, C, "k_raw")
         x_sb = []
         for load in range(N_TILES // X_LOAD_TILES):
             x_part = keep.tile([P, X_LOAD_TILES * K], BF16, name="x_sb%d" % load)
@@ -65,8 +67,6 @@ def tile_multiheadassociativememory_pa_kernel(
                 in_=x_rows[:, load * X_LOAD_TILES : (load + 1) * X_LOAD_TILES, :],
             )
             x_sb.append(x_part)
-            if load == 0:
-                k_raw = load_k_rows(shared_k_w, C, "k_raw")
 
         ident_bf16 = keep.tile([P, P], BF16)
         make_identity(nc, ident_bf16[:])
@@ -75,7 +75,7 @@ def tile_multiheadassociativememory_pa_kernel(
         minus_half = keep.tile([P, 2], F32)
         nc.gpsimd.memset(minus_half[:], -0.5)
 
-        def turn_pair(pair):
+        def turn_pair(pair, copy):
             turned = turn_psum.tile([P, PAIR * 2 * P], F32, tag="turn")
             for i in range(PAIR):
                 n = pair * PAIR + i
@@ -88,7 +88,7 @@ def tile_multiheadassociativememory_pa_kernel(
                         ident_f32[:],
                     )
             grouped = xq_pool.tile([P, PAIR * P * PACK], BF16, align_bytes=64, name="x_grouped")
-            nc.vector.tensor_copy(
+            copy(
                 out=grouped[:].bitcast(F32).rearrange("p (i r u) -> p i r u", i=PAIR, u=2),
                 in_=turned[:].rearrange("p (i u r) -> p i r u", i=PAIR, u=2),
             )
@@ -100,9 +100,9 @@ def tile_multiheadassociativememory_pa_kernel(
             nc.vector.quantize_mx(out=codes[:].bitcast(FP8X4), scales=scales[:], in_=grouped[:])
             return codes, scales
 
-        def regroup_weight(copy, raw, name):
+        def regroup_weight(raw, name):
             grouped = keep.tile([P, C, PACK], BF16, align_bytes=64, name=name)
-            copy(
+            nc.vector.tensor_copy(
                 out=grouped[:].rearrange("p (c i) t -> p c t i", i=4),
                 in_=raw[:].rearrange("p t (c i) -> p c t i", i=4),
             )
@@ -124,36 +124,39 @@ def tile_multiheadassociativememory_pa_kernel(
         for a in range(C // P):
             nc.tensor.transpose(factors_ps[:, PACK + a, :], coeff_sb[:, a, :], ident_bf16[:])
         factors = keep.tile([P, 2 * PACK, P], BF16)
-        nc.scalar.copy(out=factors[:], in_=factors_ps[:])
+        nc.vector.tensor_copy(out=factors[:], in_=factors_ps[:])
 
-        q_grouped = regroup_weight(nc.vector.tensor_copy, q_raw, "q_grouped")
-        x_grouped = turn_pair(0)
+        v_grouped = keep.tile([P, C, PACK], BF16, align_bytes=64)
+        for a in range(C // P):
+            v_w_ps = acc_psum.tile([P, P, PACK], F32, tag="acc")
+            for t in range(PACK):
+                nc.tensor.matmul(
+                    v_w_ps[:, :, t],
+                    lhsT=factors[:, t, :],
+                    rhs=factors[:, PACK + a, :],
+                    start=True,
+                    stop=True,
+                )
+            nc.scalar.copy(out=v_grouped[:, a * P : (a + 1) * P, :], in_=v_w_ps[:])
+
+        q_grouped = regroup_weight(q_raw, "q_grouped")
+        k_grouped = regroup_weight(k_raw, "k_grouped")
         q_mx = quantise_weight(q_grouped, "q")
-        x_mx = quantise_pair(x_grouped)
-
-        v_raw = keep.tile([P, PACK, C], BF16)
-        for t in range(PACK):
-            v_w_ps = qk_psum.tile([P, C], F32, tag="qk")
-            nc.tensor.matmul(
-                v_w_ps[:],
-                lhsT=factors[:, t, :],
-                rhs=factors[:, PACK:, :].rearrange("p a c -> p (a c)"),
-                start=True,
-                stop=True,
-            )
-            nc.scalar.copy(out=v_raw[:, t, :], in_=v_w_ps[:])
-
-        k_grouped = regroup_weight(nc.scalar.copy, k_raw, "k_grouped")
-        v_grouped = regroup_weight(nc.vector.tensor_copy, v_raw, "v_grouped")
         k_mx = quantise_weight(k_grouped, "k")
-        v_mx = quantise_weight(v_grouped, "v")
 
-        def product(psum, tag, weight_mx, x_codes, x_scales, i):
-            acc = psum.tile([P, C], F32, tag=tag)
+        x_mx = {}
+        x_grouped = turn_pair(0, nc.scalar.copy)
+        x_mx[0] = quantise_pair(x_grouped)
+        x_grouped = turn_pair(1, nc.vector.tensor_copy)
+        v_mx = quantise_weight(v_grouped, "v")
+        x_mx[1] = quantise_pair(x_grouped)
+
+        def product(weight_mx, pair, i):
+            acc = acc_psum.tile([P, C], F32, tag="acc")
             nc.tensor.matmul_mx(
                 out=acc[:],
-                lhsT=x_codes[:, i * P : (i + 1) * P].bitcast(FP8X4),
-                lhsT_scale=x_scales[:, i * P : (i + 1) * P],
+                lhsT=x_mx[pair][0][:, i * P : (i + 1) * P].bitcast(FP8X4),
+                lhsT_scale=x_mx[pair][1][:, i * P : (i + 1) * P],
                 rhs=weight_mx[0][:].bitcast(FP8X4),
                 rhs_scale=weight_mx[1][:],
                 start=True,
@@ -162,15 +165,13 @@ def tile_multiheadassociativememory_pa_kernel(
             return acc
 
         for pair in range(N_PAIRS):
-            if pair + 1 < N_PAIRS:
-                next_grouped = turn_pair(pair + 1)
             q_out = out_pool.tile([P, PAIR, C], F32)
             k_out = out_pool.tile([P, PAIR, C], F32)
             v_out = out_pool.tile([P, PAIR, C], F32)
             for i in range(PAIR):
-                q_ps = product(qk_psum, "qk", q_mx, x_mx[0], x_mx[1], i)
-                k_ps = product(qk_psum, "qk", k_mx, x_mx[0], x_mx[1], i)
-                v_ps = product(v_psum, "v", v_mx, x_mx[0], x_mx[1], i)
+                q_ps = product(q_mx, pair, i)
+                k_ps = product(k_mx, pair, i)
+                v_ps = product(v_mx, pair, i)
 
                 sumsq = norm_pool.tile([P, 2], F32)
                 q_sq = norm_pool.tile([P, C], BF16)
@@ -186,12 +187,14 @@ def tile_multiheadassociativememory_pa_kernel(
 
                 nc.vector.tensor_scalar_mul(out=q_out[:, i, :], in0=q_ps[:], scalar1=inv_norm[:, 0:1])
                 nc.vector.tensor_scalar_mul(out=k_out[:, i, :], in0=k_ps[:], scalar1=inv_norm[:, 1:2])
-                if i == 0 and pair + 1 < N_PAIRS:
-                    next_mx = quantise_pair(next_grouped)
+
+                if pair + AHEAD < N_PAIRS:
+                    if i == 0:
+                        x_grouped = turn_pair(pair + AHEAD, nc.vector.tensor_copy)
+                    else:
+                        x_mx[pair + AHEAD] = quantise_pair(x_grouped)
 
             tiles = slice(pair * PAIR, (pair + 1) * PAIR)
             nc.sync.dma_start(out=q_rows[:, tiles, :], in_=q_out[:])
             nc.sync.dma_start(out=k_rows[:, tiles, :], in_=k_out[:])
             nc.sync.dma_start(out=v_rows[:, tiles, :], in_=v_out[:])
-            if pair + 1 < N_PAIRS:
-                x_mx = next_mx

@@ -22,6 +22,7 @@ PAIR = 2
 N_PAIRS = N_TILES // PAIR
 AHEAD = 2
 X_LOAD_TILES = 4
+V_ON_VECTOR = 4
 EPS = 1e-12
 
 FLOPS = 3 * 2 * TOKENS * K * C + 2 * K * C * R
@@ -178,7 +179,10 @@ def tile_multiheadassociativememory_pa_kernel(
                 nc.scalar.activation(out=q_sq[:], in_=q_ps[:], func=ACT.Square, accum_out=sumsq[:, 0:1])
                 k_sq = norm_pool.tile([P, C], BF16)
                 nc.scalar.activation(out=k_sq[:], in_=k_ps[:], func=ACT.Square, accum_out=sumsq[:, 1:2])
-                nc.scalar.copy(out=v_out[:, i, :], in_=v_ps[:])
+                if (pair * PAIR + i) % V_ON_VECTOR == V_ON_VECTOR - 1:
+                    nc.vector.tensor_copy(out=v_out[:, i, :], in_=v_ps[:])
+                else:
+                    nc.scalar.copy(out=v_out[:, i, :], in_=v_ps[:])
 
                 floored = norm_pool.tile([P, 2], F32)
                 nc.gpsimd.tensor_scalar_max(out=floored[:], in0=sumsq[:], scalar1=EPS * EPS)

@@ -22,7 +22,6 @@ PAIR = 2
 N_PAIRS = N_TILES // PAIR
 AHEAD = 2
 X_LOAD_TILES = 4
-V_ON_VECTOR = 4
 EPS = 1e-12
 
 FLOPS = 3 * 2 * TOKENS * K * C + 2 * K * C * R
@@ -44,7 +43,8 @@ def tile_multiheadassociativememory_pa_kernel(
         out_pool = ctx.enter_context(tc.tile_pool(name="outp", bufs=4))
         norm_pool = ctx.enter_context(tc.tile_pool(name="norm", bufs=4))
         turn_psum = ctx.enter_context(tc.psum_pool(name="turn", bufs=1))
-        acc_psum = ctx.enter_context(tc.psum_pool(name="acc", bufs=7))
+        qk_psum = ctx.enter_context(tc.psum_pool(name="qk", bufs=6))
+        v_psum = ctx.enter_context(tc.psum_pool(name="v", bufs=1))
         ctx.enter_context(tc.manual_schedule())
 
         def load_k_rows(rows, width, name):
@@ -129,7 +129,7 @@ def tile_multiheadassociativememory_pa_kernel(
 
         v_grouped = keep.tile([P, C, PACK], BF16, align_bytes=64)
         for a in range(C // P):
-            v_w_ps = acc_psum.tile([P, P, PACK], F32, tag="acc")
+            v_w_ps = qk_psum.tile([P, P, PACK], F32, tag="qk")
             for t in range(PACK):
                 nc.tensor.matmul(
                     v_w_ps[:, :, t],
@@ -152,8 +152,8 @@ def tile_multiheadassociativememory_pa_kernel(
         v_mx = quantise_weight(v_grouped, "v")
         x_mx[1] = quantise_pair(x_grouped)
 
-        def product(weight_mx, pair, i):
-            acc = acc_psum.tile([P, C], F32, tag="acc")
+        def product(psum, tag, weight_mx, pair, i):
+            acc = psum.tile([P, C], F32, tag=tag)
             nc.tensor.matmul_mx(
                 out=acc[:],
                 lhsT=x_mx[pair][0][:, i * P : (i + 1) * P].bitcast(FP8X4),
@@ -170,33 +170,30 @@ def tile_multiheadassociativememory_pa_kernel(
             k_out = out_pool.tile([P, PAIR, C], F32)
             v_out = out_pool.tile([P, PAIR, C], F32)
             for i in range(PAIR):
-                q_ps = product(q_mx, pair, i)
-                k_ps = product(k_mx, pair, i)
-                v_ps = product(v_mx, pair, i)
+                q_ps = product(qk_psum, "qk", q_mx, pair, i)
+                k_ps = product(qk_psum, "qk", k_mx, pair, i)
+                v_ps = product(v_psum, "v", v_mx, pair, i)
 
                 sumsq = norm_pool.tile([P, 2], F32)
                 q_sq = norm_pool.tile([P, C], BF16)
                 nc.scalar.activation(out=q_sq[:], in_=q_ps[:], func=ACT.Square, accum_out=sumsq[:, 0:1])
                 k_sq = norm_pool.tile([P, C], BF16)
                 nc.scalar.activation(out=k_sq[:], in_=k_ps[:], func=ACT.Square, accum_out=sumsq[:, 1:2])
-                if (pair * PAIR + i) % V_ON_VECTOR == V_ON_VECTOR - 1:
-                    nc.vector.tensor_copy(out=v_out[:, i, :], in_=v_ps[:])
-                else:
-                    nc.scalar.copy(out=v_out[:, i, :], in_=v_ps[:])
+                nc.scalar.copy(out=v_out[:, i, :], in_=v_ps[:])
 
                 floored = norm_pool.tile([P, 2], F32)
                 nc.gpsimd.tensor_scalar_max(out=floored[:], in0=sumsq[:], scalar1=EPS * EPS)
                 inv_norm = norm_pool.tile([P, 2], F32)
                 nc.gpsimd.tensor_tensor(out=inv_norm[:], in0=floored[:], in1=minus_half[:], op=ALU.pow)
 
-                nc.vector.tensor_scalar_mul(out=q_out[:, i, :], in0=q_ps[:], scalar1=inv_norm[:, 0:1])
-                nc.vector.tensor_scalar_mul(out=k_out[:, i, :], in0=k_ps[:], scalar1=inv_norm[:, 1:2])
-
                 if pair + AHEAD < N_PAIRS:
                     if i == 0:
                         x_grouped = turn_pair(pair + AHEAD, nc.vector.tensor_copy)
                     else:
                         x_mx[pair + AHEAD] = quantise_pair(x_grouped)
+
+                nc.vector.tensor_scalar_mul(out=q_out[:, i, :], in0=q_ps[:], scalar1=inv_norm[:, 0:1])
+                nc.vector.tensor_scalar_mul(out=k_out[:, i, :], in0=k_ps[:], scalar1=inv_norm[:, 1:2])
 
             tiles = slice(pair * PAIR, (pair + 1) * PAIR)
             nc.sync.dma_start(out=q_rows[:, tiles, :], in_=q_out[:])

@@ -181,10 +181,10 @@ def tile_multiheadassociativememory_pa_kernel(
                 nc.scalar.activation(out=k_sq[:], in_=k_ps[:], func=ACT.Square, accum_out=sumsq[:, 1:2])
                 nc.scalar.copy(out=v_out[:, i, :], in_=v_ps[:])
 
-                floored = norm_pool.tile([P, 2], F32)
-                nc.gpsimd.tensor_scalar_max(out=floored[:], in0=sumsq[:], scalar1=EPS * EPS)
+                inv_sqrt = norm_pool.tile([P, 2], F32)
+                nc.gpsimd.tensor_tensor(out=inv_sqrt[:], in0=sumsq[:], in1=minus_half[:], op=ALU.pow)
                 inv_norm = norm_pool.tile([P, 2], F32)
-                nc.gpsimd.tensor_tensor(out=inv_norm[:], in0=floored[:], in1=minus_half[:], op=ALU.pow)
+                nc.vector.tensor_scalar_min(out=inv_norm[:], in0=inv_sqrt[:], scalar1=1.0 / EPS)
 
                 if pair + AHEAD < N_PAIRS:
                     if i == 0:

@@ -22,6 +22,7 @@ PAIR = 2
 N_PAIRS = N_TILES // PAIR
 AHEAD = 2
 X_LOAD_TILES = 4
+V_ON_VECTOR = 8
 EPS = 1e-12
 
 FLOPS = 3 * 2 * TOKENS * K * C + 2 * K * C * R
@@ -42,9 +43,8 @@ def tile_multiheadassociativememory_pa_kernel(
         xq_pool = ctx.enter_context(tc.tile_pool(name="xq", bufs=AHEAD + 2))
         out_pool = ctx.enter_context(tc.tile_pool(name="outp", bufs=4))
         norm_pool = ctx.enter_context(tc.tile_pool(name="norm", bufs=4))
-        turn_psum = ctx.enter_context(tc.psum_pool(name="turn", bufs=1))
         qk_psum = ctx.enter_context(tc.psum_pool(name="qk", bufs=6))
-        v_psum = ctx.enter_context(tc.psum_pool(name="v", bufs=1))
+        short_psum = ctx.enter_context(tc.psum_pool(name="short", bufs=2))
         ctx.enter_context(tc.manual_schedule())
 
         def load_k_rows(rows, width, name):
@@ -76,8 +76,8 @@ def tile_multiheadassociativememory_pa_kernel(
         minus_half = keep.tile([P, 2], F32)
         nc.gpsimd.memset(minus_half[:], -0.5)
 
-        def turn_pair(pair, copy):
-            turned = turn_psum.tile([P, PAIR * 2 * P], F32, tag="turn")
+        def transpose_pair(pair):
+            turned = short_psum.tile([P, PAIR * 2 * P], F32, tag="short")
             for i in range(PAIR):
                 n = pair * PAIR + i
                 words = x_sb[n // X_LOAD_TILES][:].bitcast(F32)
@@ -88,6 +88,9 @@ def tile_multiheadassociativememory_pa_kernel(
                         words[:, first + u * P : first + (u + 1) * P],
                         ident_f32[:],
                     )
+            return turned
+
+        def regroup_pair(turned, copy):
             grouped = xq_pool.tile([P, PAIR * P * PACK], BF16, align_bytes=64, name="x_grouped")
             copy(
                 out=grouped[:].bitcast(F32).rearrange("p (i r u) -> p i r u", i=PAIR, u=2),
@@ -119,7 +122,7 @@ def tile_multiheadassociativememory_pa_kernel(
             )
             return codes, scales
 
-        factors_ps = turn_psum.tile([P, 2 * PACK, P], BF16, tag="turn")
+        factors_ps = short_psum.tile([P, 2 * PACK, P], BF16, tag="short")
         for t in range(PACK):
             nc.tensor.transpose(factors_ps[:, t, :], basis_sb[:, t, :], ident_bf16[:])
         for a in range(C // P):
@@ -146,18 +149,20 @@ def tile_multiheadassociativememory_pa_kernel(
         k_mx = quantise_weight(k_grouped, "k")
 
         x_mx = {}
-        x_grouped = turn_pair(0, nc.scalar.copy)
+        x_grouped = regroup_pair(transpose_pair(0), nc.scalar.copy)
         x_mx[0] = quantise_pair(x_grouped)
-        x_grouped = turn_pair(1, nc.vector.tensor_copy)
+        x_grouped = regroup_pair(transpose_pair(1), nc.vector.tensor_copy)
         v_mx = quantise_weight(v_grouped, "v")
         x_mx[1] = quantise_pair(x_grouped)
 
-        def product(psum, tag, weight_mx, pair, i):
+        def product(psum, tag, weight_mx, n):
+            codes, scales = x_mx[n // PAIR]
+            cols = slice((n % PAIR) * P, (n % PAIR + 1) * P)
             acc = psum.tile([P, C], F32, tag=tag)
             nc.tensor.matmul_mx(
                 out=acc[:],
-                lhsT=x_mx[pair][0][:, i * P : (i + 1) * P].bitcast(FP8X4),
-                lhsT_scale=x_mx[pair][1][:, i * P : (i + 1) * P],
+                lhsT=codes[:, cols].bitcast(FP8X4),
+                lhsT_scale=scales[:, cols],
                 rhs=weight_mx[0][:].bitcast(FP8X4),
                 rhs_scale=weight_mx[1][:],
                 start=True,
@@ -165,37 +170,66 @@ def tile_multiheadassociativememory_pa_kernel(
             )
             return acc
 
-        for pair in range(N_PAIRS):
-            q_out = out_pool.tile([P, PAIR, C], F32)
-            k_out = out_pool.tile([P, PAIR, C], F32)
-            v_out = out_pool.tile([P, PAIR, C], F32)
-            for i in range(PAIR):
-                q_ps = product(qk_psum, "qk", q_mx, pair, i)
-                k_ps = product(qk_psum, "qk", k_mx, pair, i)
-                v_ps = product(v_psum, "v", v_mx, pair, i)
+        out_sb = {}
+        waiting = {}
+        later = {}
 
-                sumsq = norm_pool.tile([P, 2], F32)
-                q_sq = norm_pool.tile([P, C], BF16)
-                nc.scalar.activation(out=q_sq[:], in_=q_ps[:], func=ACT.Square, accum_out=sumsq[:, 0:1])
-                k_sq = norm_pool.tile([P, C], BF16)
-                nc.scalar.activation(out=k_sq[:], in_=k_ps[:], func=ACT.Square, accum_out=sumsq[:, 1:2])
-                nc.scalar.copy(out=v_out[:, i, :], in_=v_ps[:])
+        def multiply_and_sum(n):
+            pair, i = divmod(n, PAIR)
+            if i == 0:
+                q_out = out_pool.tile([P, PAIR, C], F32)
+                k_out = out_pool.tile([P, PAIR, C], F32)
+                v_out = out_pool.tile([P, PAIR, C], F32)
+                out_sb[pair] = (q_out, k_out, v_out)
+            q_ps = product(qk_psum, "qk", q_mx, n)
+            k_ps = product(qk_psum, "qk", k_mx, n)
+            v_ps = product(short_psum, "short", v_mx, n)
+            if i == 0 and pair + AHEAD < N_PAIRS:
+                later["turned"] = transpose_pair(pair + AHEAD)
 
-                inv_sqrt = norm_pool.tile([P, 2], F32)
-                nc.gpsimd.tensor_tensor(out=inv_sqrt[:], in0=sumsq[:], in1=minus_half[:], op=ALU.pow)
+            sumsq = norm_pool.tile([P, 2], F32)
+            q_sq = norm_pool.tile([P, C], BF16)
+            nc.scalar.activation(out=q_sq[:], in_=q_ps[:], func=ACT.Square, accum_out=sumsq[:, 0:1])
+            k_sq = norm_pool.tile([P, C], BF16)
+            nc.scalar.activation(out=k_sq[:], in_=k_ps[:], func=ACT.Square, accum_out=sumsq[:, 1:2])
+            if n % V_ON_VECTOR == V_ON_VECTOR - 1:
+                nc.vector.tensor_copy(out=out_sb[pair][2][:, i, :], in_=v_ps[:])
+            else:
+                nc.scalar.copy(out=out_sb[pair][2][:, i, :], in_=v_ps[:])
+            inv_sqrt = norm_pool.tile([P, 2], F32)
+            nc.gpsimd.tensor_tensor(out=inv_sqrt[:], in0=sumsq[:], in1=minus_half[:], op=ALU.pow)
+            waiting[n] = (q_ps, k_ps, inv_sqrt)
+
+        def prepare_later_pair(n):
+            pair, i = divmod(n, PAIR)
+            if pair + AHEAD < N_PAIRS:
+                if i == 0:
+                    later["grouped"] = regroup_pair(later["turned"], nc.vector.tensor_copy)
+                else:
+                    x_mx[pair + AHEAD] = quantise_pair(later["grouped"])
+
+        def store(n, count):
+            q_out, k_out, v_out = out_sb[n // PAIR]
+            tiles = slice(n + 1 - count, n + 1)
+            part = slice(n % PAIR + 1 - count, n % PAIR + 1)
+            nc.sync.dma_start(out=v_rows[:, tiles, :], in_=v_out[:, part, :])
+            nc.sync.dma_start(out=q_rows[:, tiles, :], in_=q_out[:, part, :])
+            nc.sync.dma_start(out=k_rows[:, tiles, :], in_=k_out[:, part, :])
+
+        for n in range(N_TILES + 1):
+            if n < N_TILES:
+                multiply_and_sum(n)
+            if n > 0:
+                q_ps, k_ps, inv_sqrt = waiting[n - 1]
                 inv_norm = norm_pool.tile([P, 2], F32)
                 nc.vector.tensor_scalar_min(out=inv_norm[:], in0=inv_sqrt[:], scalar1=1.0 / EPS)
-
-                if pair + AHEAD < N_PAIRS:
-                    if i == 0:
-                        x_grouped = turn_pair(pair + AHEAD, nc.vector.tensor_copy)
-                    else:
-                        x_mx[pair + AHEAD] = quantise_pair(x_grouped)
-
-                nc.vector.tensor_scalar_mul(out=q_out[:, i, :], in0=q_ps[:], scalar1=inv_norm[:, 0:1])
-                nc.vector.tensor_scalar_mul(out=k_out[:, i, :], in0=k_ps[:], scalar1=inv_norm[:, 1:2])
-
-            tiles = slice(pair * PAIR, (pair + 1) * PAIR)
-            nc.sync.dma_start(out=q_rows[:, tiles, :], in_=q_out[:])
-            nc.sync.dma_start(out=k_rows[:, tiles, :], in_=k_out[:])
-            nc.sync.dma_start(out=v_rows[:, tiles, :], in_=v_out[:])
+            if n < N_TILES:
+                prepare_later_pair(n)
+            if n > 0:
+                pair, i = divmod(n - 1, PAIR)
+                nc.vector.tensor_scalar_mul(out=out_sb[pair][0][:, i, :], in0=q_ps[:], scalar1=inv_norm[:, 0:1])
+                nc.vector.tensor_scalar_mul(out=out_sb[pair][1][:, i, :], in0=k_ps[:], scalar1=inv_norm[:, 1:2])
+                if pair == 0 or pair == N_PAIRS - 1:
+                    store(n - 1, 1)
+                elif i == PAIR - 1:
+                    store(n - 1, PAIR)

from contextlib import ExitStack

import concourse.mybir as mybir
from concourse.masks import make_identity

F32 = mybir.dt.float32
BF16 = mybir.dt.bfloat16
U32 = mybir.dt.uint32
U8 = mybir.dt.uint8
FP8X4 = mybir.dt.float8_e4m3fn_x4
ALU = mybir.AluOpType
ACT = mybir.ActivationFunctionType

P = 128
PACK = 4
K = P * PACK
C = 512
R = 128
TOKENS = 4 * 1024
N_TILES = TOKENS // P
PAIR = 2
N_PAIRS = N_TILES // PAIR
AHEAD = 2
X_LOAD_TILES = 4
V_ON_VECTOR = 8
EPS = 1e-12

FLOPS = 3 * 2 * TOKENS * K * C + 2 * K * C * R


def tile_multiheadassociativememory_pa_kernel(
    tc, x, basis, shared_q_w, shared_k_w, v_coeffs, out_0, out_1, out_2
):
    nc = tc.nc

    x_rows = x.flatten_outer_dims().rearrange("(p n) k -> p n k", n=N_TILES)
    q_rows = out_0.flatten_outer_dims().rearrange("(p n) c -> p n c", n=N_TILES)
    k_rows = out_1.flatten_outer_dims().rearrange("(p n) c -> p n c", n=N_TILES)
    v_rows = out_2.flatten_outer_dims().rearrange("(p n) c -> p n c", n=N_TILES)

    with ExitStack() as ctx:
        keep = ctx.enter_context(tc.tile_pool(name="keep", bufs=1))
        xq_pool = ctx.enter_context(tc.tile_pool(name="xq", bufs=AHEAD + 2))
        out_pool = ctx.enter_context(tc.tile_pool(name="outp", bufs=4))
        norm_pool = ctx.enter_context(tc.tile_pool(name="norm", bufs=4))
        qk_psum = ctx.enter_context(tc.psum_pool(name="qk", bufs=6))
        short_psum = ctx.enter_context(tc.psum_pool(name="short", bufs=2))
        ctx.enter_context(tc.manual_schedule())

        def load_k_rows(rows, width, name):
            raw = keep.tile([P, PACK, width], BF16, name=name)
            nc.sync.dma_start(
                out=raw[:].rearrange("p (u e) w -> p u e w", u=2),
                in_=rows.rearrange("(u p e) w -> p u e w", u=2, e=2),
            )
            return raw

        basis_sb = load_k_rows(basis, R, "basis_sb")
        coeff_sb = keep.tile([P, C // P, R], BF16)
        nc.sync.dma_start(out=coeff_sb[:], in_=v_coeffs.rearrange("(a p) r -> p a r", p=P))
        q_raw = load_k_rows(shared_q_w, C, "q_raw")
        k_raw = load_k_rows(shared_k_w, C, "k_raw")
        x_sb = []
        for load in range(N_TILES // X_LOAD_TILES):
            x_part = keep.tile([P, X_LOAD_TILES * K], BF16, name="x_sb%d" % load)
            nc.sync.dma_start(
                out=x_part[:].rearrange("p (n k) -> p n k", k=K),
                in_=x_rows[:, load * X_LOAD_TILES : (load + 1) * X_LOAD_TILES, :],
            )
            x_sb.append(x_part)

        ident_bf16 = keep.tile([P, P], BF16)
        make_identity(nc, ident_bf16[:])
        ident_f32 = keep.tile([P, P], F32)
        make_identity(nc, ident_f32[:])
        minus_half = keep.tile([P, 2], F32)
        nc.gpsimd.memset(minus_half[:], -0.5)

        def transpose_pair(pair):
            turned = short_psum.tile([P, PAIR * 2 * P], F32, tag="short")
            for i in range(PAIR):
                n = pair * PAIR + i
                words = x_sb[n // X_LOAD_TILES][:].bitcast(F32)
                first = (n % X_LOAD_TILES) * (K // 2)
                for u in range(2):
                    nc.tensor.transpose(
                        turned[:, (2 * i + u) * P : (2 * i + u + 1) * P],
                        words[:, first + u * P : first + (u + 1) * P],
                        ident_f32[:],
                    )
            return turned

        def regroup_pair(turned, copy):
            grouped = xq_pool.tile([P, PAIR * P * PACK], BF16, align_bytes=64, name="x_grouped")
            copy(
                out=grouped[:].bitcast(F32).rearrange("p (i r u) -> p i r u", i=PAIR, u=2),
                in_=turned[:].rearrange("p (i u r) -> p i r u", i=PAIR, u=2),
            )
            return grouped

        def quantise_pair(grouped):
            codes = xq_pool.tile([P, PAIR * P], U32, align_bytes=64, name="x_codes")
            scales = xq_pool.tile([P, PAIR * P], U8, align_bytes=64, name="x_scales")
            nc.vector.quantize_mx(out=codes[:].bitcast(FP8X4), scales=scales[:], in_=grouped[:])
            return codes, scales

        def regroup_weight(raw, name):
            grouped = keep.tile([P, C, PACK], BF16, align_bytes=64, name=name)
            nc.vector.tensor_copy(
                out=grouped[:].rearrange("p (c i) t -> p c t i", i=4),
                in_=raw[:].rearrange("p t (c i) -> p c t i", i=4),
            )
            return grouped

        def quantise_weight(grouped, name):
            codes = keep.tile([P, C], U32, align_bytes=64, name=name + "_codes")
            scales = keep.tile([P, C], U8, align_bytes=64, name=name + "_scales")
            nc.vector.quantize_mx(
                out=codes[:].bitcast(FP8X4),
                scales=scales[:],
                in_=grouped[:].rearrange("p c t -> p (c t)"),
            )
            return codes, scales

        factors_ps = short_psum.tile([P, 2 * PACK, P], BF16, tag="short")
        for t in range(PACK):
            nc.tensor.transpose(factors_ps[:, t, :], basis_sb[:, t, :], ident_bf16[:])
        for a in range(C // P):
            nc.tensor.transpose(factors_ps[:, PACK + a, :], coeff_sb[:, a, :], ident_bf16[:])
        factors = keep.tile([P, 2 * PACK, P], BF16)
        nc.vector.tensor_copy(out=factors[:], in_=factors_ps[:])

        v_grouped = keep.tile([P, C, PACK], BF16, align_bytes=64)
        for a in range(C // P):
            v_w_ps = qk_psum.tile([P, P, PACK], F32, tag="qk")
            for t in range(PACK):
                nc.tensor.matmul(
                    v_w_ps[:, :, t],
                    lhsT=factors[:, t, :],
                    rhs=factors[:, PACK + a, :],
                    start=True,
                    stop=True,
                )
            nc.scalar.copy(out=v_grouped[:, a * P : (a + 1) * P, :], in_=v_w_ps[:])

        q_grouped = regroup_weight(q_raw, "q_grouped")
        k_grouped = regroup_weight(k_raw, "k_grouped")
        q_mx = quantise_weight(q_grouped, "q")
        k_mx = quantise_weight(k_grouped, "k")

        x_mx = {}
        x_grouped = regroup_pair(transpose_pair(0), nc.scalar.copy)
        x_mx[0] = quantise_pair(x_grouped)
        x_grouped = regroup_pair(transpose_pair(1), nc.vector.tensor_copy)
        v_mx = quantise_weight(v_grouped, "v")
        x_mx[1] = quantise_pair(x_grouped)

        def product(psum, tag, weight_mx, n):
            codes, scales = x_mx[n // PAIR]
            cols = slice((n % PAIR) * P, (n % PAIR + 1) * P)
            acc = psum.tile([P, C], F32, tag=tag)
            nc.tensor.matmul_mx(
                out=acc[:],
                lhsT=codes[:, cols].bitcast(FP8X4),
                lhsT_scale=scales[:, cols],
                rhs=weight_mx[0][:].bitcast(FP8X4),
                rhs_scale=weight_mx[1][:],
                start=True,
                stop=True,
            )
            return acc

        out_sb = {}
        waiting = {}
        later = {}

        def multiply_and_sum(n):
            pair, i = divmod(n, PAIR)
            if i == 0:
                q_out = out_pool.tile([P, PAIR, C], F32)
                k_out = out_pool.tile([P, PAIR, C], F32)
                v_out = out_pool.tile([P, PAIR, C], F32)
                out_sb[pair] = (q_out, k_out, v_out)
            q_ps = product(qk_psum, "qk", q_mx, n)
            k_ps = product(qk_psum, "qk", k_mx, n)
            v_ps = product(short_psum, "short", v_mx, n)
            if i == 0 and pair + AHEAD < N_PAIRS:
                later["turned"] = transpose_pair(pair + AHEAD)

            sumsq = norm_pool.tile([P, 2], F32)
            q_sq = norm_pool.tile([P, C], BF16)
            nc.scalar.activation(out=q_sq[:], in_=q_ps[:], func=ACT.Square, accum_out=sumsq[:, 0:1])
            k_sq = norm_pool.tile([P, C], BF16)
            nc.scalar.activation(out=k_sq[:], in_=k_ps[:], func=ACT.Square, accum_out=sumsq[:, 1:2])
            if n % V_ON_VECTOR == V_ON_VECTOR - 1:
                nc.vector.tensor_copy(out=out_sb[pair][2][:, i, :], in_=v_ps[:])
            else:
                nc.scalar.copy(out=out_sb[pair][2][:, i, :], in_=v_ps[:])
            inv_sqrt = norm_pool.tile([P, 2], F32)
            nc.gpsimd.tensor_tensor(out=inv_sqrt[:], in0=sumsq[:], in1=minus_half[:], op=ALU.pow)
            waiting[n] = (q_ps, k_ps, inv_sqrt)

        def prepare_later_pair(n):
            pair, i = divmod(n, PAIR)
            if pair + AHEAD < N_PAIRS:
                if i == 0:
                    later["grouped"] = regroup_pair(later["turned"], nc.vector.tensor_copy)
                else:
                    x_mx[pair + AHEAD] = quantise_pair(later["grouped"])

        def store(n, count):
            q_out, k_out, v_out = out_sb[n // PAIR]
            tiles = slice(n + 1 - count, n + 1)
            part = slice(n % PAIR + 1 - count, n % PAIR + 1)
            nc.sync.dma_start(out=v_rows[:, tiles, :], in_=v_out[:, part, :])
            nc.sync.dma_start(out=q_rows[:, tiles, :], in_=q_out[:, part, :])
            nc.sync.dma_start(out=k_rows[:, tiles, :], in_=k_out[:, part, :])

        for n in range(N_TILES + 1):
            if n < N_TILES:
                multiply_and_sum(n)
            if n > 0:
                q_ps, k_ps, inv_sqrt = waiting[n - 1]
                inv_norm = norm_pool.tile([P, 2], F32)
                nc.vector.tensor_scalar_min(out=inv_norm[:], in0=inv_sqrt[:], scalar1=1.0 / EPS)
            if n < N_TILES:
                prepare_later_pair(n)
            if n > 0:
                pair, i = divmod(n - 1, PAIR)
                nc.vector.tensor_scalar_mul(out=out_sb[pair][0][:, i, :], in0=q_ps[:], scalar1=inv_norm[:, 0:1])
                nc.vector.tensor_scalar_mul(out=out_sb[pair][1][:, i, :], in0=k_ps[:], scalar1=inv_norm[:, 1:2])
                if pair == 0 or pair == N_PAIRS - 1:
                    store(n - 1, 1)
                elif i == PAIR - 1:
                    store(n - 1, PAIR)
